import numpy as np
import ml_dtypes


def mxq(x, axis, fmt="e4m3"):
    dtype, down = {"e4m3": (ml_dtypes.float8_e4m3fn, 7), "e5m2": (ml_dtypes.float8_e5m2, 14)}[fmt]
    v = np.moveaxis(np.asarray(x, np.float32).astype(ml_dtypes.bfloat16).astype(np.float64), axis, -1)
    blocks = v.reshape(v.shape[:-1] + (-1, 32))
    amax = np.abs(blocks).max(-1, keepdims=True)
    byte = np.maximum(np.where(amax > 0, np.frexp(amax)[1] - 1 + 127, 0) - down, 1)
    scale = np.exp2(byte - 127.0)
    codes = (blocks / scale).astype(np.float32).astype(dtype).astype(np.float64)
    return np.moveaxis((codes * scale).reshape(v.shape), -1, axis)


WIDE = False


def mx_kscale(k):
    if not WIDE:
        return np.ones(k)
    levels = np.array([10, -10, 5, -5, 0])
    a = np.random.permutation(np.resize(levels, k // 512 * 4)).reshape(k // 512, 4)
    idx = np.arange(k)
    return np.exp2(a[idx // 512, idx % 128 // 32])


BF16 = ml_dtypes.bfloat16


def bf(x):
    return np.asarray(x, np.float32).astype(BF16)


def f64(x):
    return np.asarray(x).astype(np.float64)


B, L, D, H, KV, HD, QB = 4, 2048, 1024, 2, 2, 64, 512
EPS_RMS = 1e-6
EPS_NORM = 1e-12


def rmsnorm(x, w):
    var = np.mean(np.square(x), axis=-1, keepdims=True)
    return x * (1.0 / np.sqrt(var + EPS_RMS)) * w


def l2norm(x):
    n = np.sqrt(np.sum(np.square(x), axis=-1, keepdims=True))
    return x / np.maximum(n, EPS_NORM)


def heads(y, n):
    return y.reshape(B, L, n, HD).transpose(0, 2, 1, 3)


def setup_inputs():
    s = mx_kscale(D)
    c = 1.0 / np.sqrt(D)
    return {"x": bf(np.random.standard_normal((B, L, D)) * np.exp(0.5 * np.random.standard_normal((B, L, 1)))),
            "norm_w": bf((1.0 + 0.1 * np.random.standard_normal(D)) * s),
            "Wq": bf(np.random.standard_normal((D, H * HD)) * c / s[:, None]),
            "Wk": bf(np.random.standard_normal((D, KV * HD)) * c / s[:, None]),
            "Wv": bf(np.random.standard_normal((D, KV * HD)) * c / s[:, None])}


def reference(x, norm_w, Wq, Wk, Wv):
    h = mxq(rmsnorm(f64(x), f64(norm_w)), 2, "e4m3")
    q = heads(h @ mxq(f64(Wq), 0, "e4m3"), H)
    k = heads(h @ mxq(f64(Wk), 0, "e4m3"), KV)
    v = heads(h @ mxq(f64(Wv), 0, "e4m3"), KV)
    return l2norm(q), l2norm(k), v

@@ -1,0 +1,200 @@
+from contextlib import ExitStack
+
+import concourse.mybir as mybir
+from concourse.masks import make_identity
+
+F32 = mybir.dt.float32
+BF16 = mybir.dt.bfloat16
+U32 = mybir.dt.uint32
+U8 = mybir.dt.uint8
+FP8X4 = mybir.dt.float8_e4m3fn_x4
+ACT = mybir.ActivationFunctionType
+ALU = mybir.AluOpType
+
+P = 128
+B, L, D = 4, 2048, 1024
+HD = 64
+J = L // P
+GROUP = 4
+BUNCH = 2
+N_GROUPS = B * J // GROUP
+N_BUNCHES = B * J // BUNCH
+FLOPS = 2 * B * L * D * 384
+
+
+def tile_sharedglobalattention_pa_t_kernel(tc, x, norm_w, Wq, Wk, Wv, out_0, out_1, out_2):
+    nc = tc.nc
+    with ExitStack() as ctx:
+        const = ctx.enter_context(tc.tile_pool(name="const", bufs=1))
+        xpool = ctx.enter_context(tc.tile_pool(name="xin", bufs=4))
+        junkp = ctx.enter_context(tc.tile_pool(name="junk", bufs=2))
+        small = ctx.enter_context(tc.tile_pool(name="small", bufs=4))
+        ypool = ctx.enter_context(tc.tile_pool(name="ytok", bufs=6))
+        gpool = ctx.enter_context(tc.tile_pool(name="grouped", bufs=3))
+        opool = ctx.enter_context(tc.tile_pool(name="outs", bufs=3))
+        ps_t = ctx.enter_context(tc.psum_pool(name="ps_t", bufs=4))
+        ps_o = ctx.enter_context(tc.psum_pool(name="ps_o", bufs=2))
+
+        xv = [x[b].rearrange("(p j) d -> p j d", j=J) for b in range(B)]
+        outs = (out_0, out_1, out_2)
+        ov = [[o[b].rearrange("n (p j) d -> p n j d", j=J) for b in range(B)] for o in outs]
+
+        xg = {}
+
+        def load(g):
+            b, j0 = divmod(g * GROUP, J)
+            t = xpool.tile([P, GROUP, D], BF16, name="xg")
+            xg[g] = t
+            if g == 0:
+                for jj in range(GROUP):
+                    nc.sync.dma_start(out=t[:, jj : jj + 1, :], in_=xv[b][:, j0 + jj : j0 + jj + 1, :])
+            else:
+                nc.sync.dma_start(out=t[:], in_=xv[b][:, j0 : j0 + GROUP, :])
+
+        load(0)
+
+        eps_t = const.tile([P, 1], F32, name="eps_t")
+        nc.vector.memset(eps_t[:], 1e-6)
+        warm = const.tile([P, 1], F32, name="warm")
+        nc.scalar.activation(out=warm[:], in_=eps_t[:], func=ACT.Sqrt)
+        ident = const.tile([P, P], F32, name="ident")
+        make_identity(nc, ident[:])
+
+        nw_rows = const.tile([P, P], BF16, name="nw_rows")
+        nc.gpsimd.memset(nw_rows[:], 0.0)
+        nc.scalar.dma_start(out=nw_rows[0:8, :], in_=norm_w.rearrange("(c p) -> c p", p=P))
+        wraw = const.tile([P, 8, 384], BF16, name="wraw")
+        for m, w in enumerate((Wq, Wk, Wv)):
+            nc.scalar.dma_start(
+                out=wraw[:, :, m * P : (m + 1) * P], in_=w.rearrange("(c p) n -> p c n", p=P)
+            )
+        nw_f = const.tile([P, P], F32, name="nw_f")
+        nc.vector.tensor_copy(out=nw_f[:], in_=nw_rows[:])
+        nw_ps = ps_t.tile([P, 4, P], F32, name="yT")
+        nc.tensor.transpose(out=nw_ps[:, 0, :], in_=nw_f[:], identity=ident[:])
+        w4 = const.tile([P, 8], F32, name="w4")
+        nc.vector.tensor_copy(out=w4[:], in_=nw_ps[:, 0, 0:8])
+
+        wqk_g = const.tile([P, 2, 256, 4], BF16, name="wqk_g", align_bytes=64)
+        wv_g = const.tile([P, 2, P, 4], BF16, name="wv_g", align_bytes=64)
+        wr = wraw[:].rearrange("p (g t) n -> p g t n", t=4)
+        for g in range(2):
+            nc.vector.tensor_copy(out=wqk_g[:, g], in_=wr[:, g, :, 0:256].rearrange("p t n -> p n t"))
+            nc.vector.tensor_copy(out=wv_g[:, g], in_=wr[:, g, :, 256:384].rearrange("p t n -> p n t"))
+        wqk_c = const.tile([P, 512], U32, name="wqk_c", align_bytes=64)
+        wqk_s = const.tile([P, 512], U8, name="wqk_s", align_bytes=64)
+        wv_c = const.tile([P, 256], U32, name="wv_c", align_bytes=64)
+        wv_s = const.tile([P, 256], U8, name="wv_s", align_bytes=64)
+        nc.vector.quantize_mx(
+            out=wqk_c[:].bitcast(FP8X4), scales=wqk_s[:], in_=wqk_g[:].rearrange("p g n t -> p (g n t)")
+        )
+        nc.vector.quantize_mx(
+            out=wv_c[:].bitcast(FP8X4), scales=wv_s[:], in_=wv_g[:].rearrange("p g n t -> p (g n t)")
+        )
+
+        rstd = {}
+        otile = {}
+
+        def stats(g):
+            ss = small.tile([P, GROUP], F32, name="ss")
+            for jj in range(GROUP):
+                junk = junkp.tile([P, D], BF16, name="junk")
+                nc.scalar.activation(
+                    out=junk[:], in_=xg[g][:, jj, :], func=ACT.Square, accum_out=ss[:, jj : jj + 1]
+                )
+            sd = small.tile([P, GROUP], F32, name="sd")
+            nc.scalar.activation(out=sd[:], in_=ss[:], func=ACT.Sqrt, scale=1.0 / D, bias=eps_t[:, 0:1])
+            r = small.tile([P, GROUP], F32, name="rstd")
+            nc.vector.reciprocal(out=r[:], in_=sd[:])
+            rstd[g] = r
+
+        def bunch(bn):
+            g, half = divmod(bn, GROUP // BUNCH)
+            grp = gpool.tile([P, BUNCH * 2 * 512], BF16, name="grp", align_bytes=64)
+            for i in range(BUNCH):
+                jj = half * BUNCH + i
+                y = ypool.tile([P, D], F32, name="y")
+                nc.gpsimd.tensor_scalar(
+                    out=y[:],
+                    in0=xg[g][:, jj, :],
+                    scalar1=rstd[g][:, jj : jj + 1],
+                    scalar2=0.0,
+                    op0=ALU.mult,
+                    op1=ALU.add,
+                )
+                for c in range(2):
+                    yT = ps_t.tile([P, 4, P], F32, name="yT")
+                    for t in range(4):
+                        k0 = (c * 4 + t) * P
+                        nc.tensor.transpose(out=yT[:, t, :], in_=y[:, k0 : k0 + P], identity=ident[:])
+                    col = (i * 2 + c) * 512
+                    nc.vector.tensor_tensor(
+                        out=grp[:, col : col + 512].rearrange("p (k t) -> p k t", t=4),
+                        in0=yT[:].rearrange("p t k -> p k t"),
+                        in1=w4[:, c * 4 : (c + 1) * 4].unsqueeze(1).to_broadcast([P, P, 4]),
+                        op=ALU.mult,
+                    )
+            codes = gpool.tile([P, BUNCH * 2 * P], U32, name="codes", align_bytes=64)
+            scl = gpool.tile([P, BUNCH * 2 * P], U8, name="scl", align_bytes=64)
+            nc.vector.quantize_mx(out=codes[:].bitcast(FP8X4), scales=scl[:], in_=grp[:])
+
+            qk = ps_o.tile([P, BUNCH, 256], F32, name="qk")
+            vp = ps_o.tile([P, BUNCH, P], F32, name="vp")
+            for i in range(BUNCH):
+                for dst, wc, ws, n in ((qk, wqk_c, wqk_s, 256), (vp, wv_c, wv_s, P)):
+                    for c in range(2):
+                        col = (i * 2 + c) * P
+                        nc.tensor.matmul_mx(
+                            out=dst[:, i, :],
+                            lhsT=codes[:, col : col + P].bitcast(FP8X4),
+                            lhsT_scale=scl[:, col : col + P],
+                            rhs=wc[:, c * n : (c + 1) * n].bitcast(FP8X4),
+                            rhs_scale=ws[:, c * n : (c + 1) * n],
+                            start=(c == 0),
+                            stop=(c == 1),
+                        )
+
+            if half == 0:
+                otile[g] = opool.tile([P, 6, GROUP, HD], F32, name="otile")
+            o = otile[g]
+            j0 = half * BUNCH
+            ssq = small.tile([P, BUNCH * 4], F32, name="ssq")
+            for i in range(BUNCH):
+                for w in range(4):
+                    junk2 = junkp.tile([P, HD], BF16, name="junk2")
+                    nc.scalar.activation(
+                        out=junk2[:],
+                        in_=qk[:, i, w * HD : (w + 1) * HD],
+                        func=ACT.Square,
+                        accum_out=ssq[:, i * 4 + w : i * 4 + w + 1],
+                    )
+            nc.scalar.copy(
+                out=o[:, 4:6, j0 : j0 + BUNCH, :], in_=vp[:].rearrange("p i (w d) -> p w i d", d=HD)
+            )
+            ssc = small.tile([P, BUNCH * 4], F32, name="ssc")
+            nc.vector.tensor_scalar_max(out=ssc[:], in0=ssq[:], scalar1=1e-24)
+            nrm = small.tile([P, BUNCH * 4], F32, name="nrm")
+            nc.scalar.activation(out=nrm[:], in_=ssc[:], func=ACT.Sqrt)
+            rn = small.tile([P, BUNCH * 4], F32, name="rn")
+            nc.vector.reciprocal(out=rn[:], in_=nrm[:])
+            nc.vector.tensor_tensor(
+                out=o[:, 0:4, j0 : j0 + BUNCH, :],
+                in0=qk[:].rearrange("p i (w d) -> p w i d", d=HD),
+                in1=rn[:].rearrange("p (i w) -> p w i", w=4).unsqueeze(3).to_broadcast([P, 4, BUNCH, HD]),
+                op=ALU.mult,
+            )
+
+        def store(g):
+            b, j0 = divmod(g * GROUP, J)
+            for m in range(3):
+                nc.sync.dma_start(
+                    out=ov[m][b][:, :, j0 : j0 + GROUP, :], in_=otile[g][:, 2 * m : 2 * m + 2, :, :]
+                )
+
+        for g in range(N_GROUPS):
+            if g + 1 < N_GROUPS:
+                load(g + 1)
+            stats(g)
+            for half in range(GROUP // BUNCH):
+                bunch(g * (GROUP // BUNCH) + half)
+            store(g)

@@ -16,10 +16,13 @@ B, L, D = 4, 2048, 1024
 HD = 64
 J = L // P
 GROUP = 4
-BUNCH = 2
-N_GROUPS = B * J // GROUP
-N_BUNCHES = B * J // BUNCH
+N_TILES = B * J
+N_GROUPS = N_TILES // GROUP
 FLOPS = 2 * B * L * D * 384
+
+LOAD_LEAD = 10
+SUMSQ_LEAD = 6
+Y_LEAD = 3
 
 
 def tile_sharedglobalattention_pa_t_kernel(tc, x, norm_w, Wq, Wk, Wv, out_0, out_1, out_2):
@@ -28,18 +31,19 @@ def tile_sharedglobalattention_pa_t_kernel(tc, x, norm_w, Wq, Wk, Wv, out_0, out
         const = ctx.enter_context(tc.tile_pool(name="const", bufs=1))
         xpool = ctx.enter_context(tc.tile_pool(name="xin", bufs=4))
         junkp = ctx.enter_context(tc.tile_pool(name="junk", bufs=2))
-        small = ctx.enter_context(tc.tile_pool(name="small", bufs=4))
-        ypool = ctx.enter_context(tc.tile_pool(name="ytok", bufs=6))
+        small = ctx.enter_context(tc.tile_pool(name="small", bufs=8))
+        ypool = ctx.enter_context(tc.tile_pool(name="ytok", bufs=5))
         gpool = ctx.enter_context(tc.tile_pool(name="grouped", bufs=3))
         opool = ctx.enter_context(tc.tile_pool(name="outs", bufs=3))
         ps_t = ctx.enter_context(tc.psum_pool(name="ps_t", bufs=4))
-        ps_o = ctx.enter_context(tc.psum_pool(name="ps_o", bufs=2))
+        ps_o = ctx.enter_context(tc.psum_pool(name="ps_o", bufs=4))
+        ctx.enter_context(tc.manual_schedule())
 
         xv = [x[b].rearrange("(p j) d -> p j d", j=J) for b in range(B)]
         outs = (out_0, out_1, out_2)
         ov = [[o[b].rearrange("n (p j) d -> p n j d", j=J) for b in range(B)] for o in outs]
 
-        xg = {}
+        xg, ss, sd, rstd, ys, yts, grps, cds, pos, ssqs, rns, otile = {}, {}, {}, {}, {}, {}, {}, {}, {}, {}, {}, {}
 
         def load(g):
             b, j0 = divmod(g * GROUP, J)
@@ -53,134 +57,165 @@ def tile_sharedglobalattention_pa_t_kernel(tc, x, norm_w, Wq, Wk, Wv, out_0, out
 
         load(0)
 
-        eps_t = const.tile([P, 1], F32, name="eps_t")
-        nc.vector.memset(eps_t[:], 1e-6)
-        warm = const.tile([P, 1], F32, name="warm")
-        nc.scalar.activation(out=warm[:], in_=eps_t[:], func=ACT.Sqrt)
-        ident = const.tile([P, P], F32, name="ident")
-        make_identity(nc, ident[:])
-
         nw_rows = const.tile([P, P], BF16, name="nw_rows")
         nc.gpsimd.memset(nw_rows[:], 0.0)
-        nc.scalar.dma_start(out=nw_rows[0:8, :], in_=norm_w.rearrange("(c p) -> c p", p=P))
         wraw = const.tile([P, 8, 384], BF16, name="wraw")
         for m, w in enumerate((Wq, Wk, Wv)):
             nc.scalar.dma_start(
                 out=wraw[:, :, m * P : (m + 1) * P], in_=w.rearrange("(c p) n -> p c n", p=P)
             )
-        nw_f = const.tile([P, P], F32, name="nw_f")
-        nc.vector.tensor_copy(out=nw_f[:], in_=nw_rows[:])
-        nw_ps = ps_t.tile([P, 4, P], F32, name="yT")
-        nc.tensor.transpose(out=nw_ps[:, 0, :], in_=nw_f[:], identity=ident[:])
+        nc.scalar.dma_start(out=nw_rows[0:8, :], in_=norm_w.rearrange("(c p) -> c p", p=P))
+        eps_t = const.tile([P, 1], F32, name="eps_t")
+        nc.vector.memset(eps_t[:], 1e-6)
+        tiny_p = const.tile([P, 1], F32, name="tiny_p")
+        nc.vector.memset(tiny_p[:], 1e-24)
+        tiny_n = const.tile([P, 1], F32, name="tiny_n")
+        nc.vector.memset(tiny_n[:], -1e-24)
+        warm = const.tile([P, 1], F32, name="warm")
+        nc.scalar.activation(out=warm[:], in_=eps_t[:], func=ACT.Sqrt)
+        ident = const.tile([P, P], F32, name="ident")
+        make_identity(nc, ident[:])
+        w_g = const.tile([P, 2, 512, 4], BF16, name="w_g", align_bytes=64)
+        nc.gpsimd.memset(w_g[:, :, 384:512, :], 0.0)
+        w_c = const.tile([P, 1024], U32, name="w_c", align_bytes=64)
+        w_s = const.tile([P, 1024], U8, name="w_s", align_bytes=64)
         w4 = const.tile([P, 8], F32, name="w4")
-        nc.vector.tensor_copy(out=w4[:], in_=nw_ps[:, 0, 0:8])
 
-        wqk_g = const.tile([P, 2, 256, 4], BF16, name="wqk_g", align_bytes=64)
-        wv_g = const.tile([P, 2, P, 4], BF16, name="wv_g", align_bytes=64)
-        wr = wraw[:].rearrange("p (g t) n -> p g t n", t=4)
-        for g in range(2):
-            nc.vector.tensor_copy(out=wqk_g[:, g], in_=wr[:, g, :, 0:256].rearrange("p t n -> p n t"))
-            nc.vector.tensor_copy(out=wv_g[:, g], in_=wr[:, g, :, 256:384].rearrange("p t n -> p n t"))
-        wqk_c = const.tile([P, 512], U32, name="wqk_c", align_bytes=64)
-        wqk_s = const.tile([P, 512], U8, name="wqk_s", align_bytes=64)
-        wv_c = const.tile([P, 256], U32, name="wv_c", align_bytes=64)
-        wv_s = const.tile([P, 256], U8, name="wv_s", align_bytes=64)
-        nc.vector.quantize_mx(
-            out=wqk_c[:].bitcast(FP8X4), scales=wqk_s[:], in_=wqk_g[:].rearrange("p g n t -> p (g n t)")
-        )
-        nc.vector.quantize_mx(
-            out=wv_c[:].bitcast(FP8X4), scales=wv_s[:], in_=wv_g[:].rearrange("p g n t -> p (g n t)")
-        )
+        def prep_norm_w():
+            nw_f = const.tile([P, P], F32, name="nw_f")
+            nc.vector.tensor_copy(out=nw_f[:], in_=nw_rows[:])
+            nw_ps = ps_t.tile([P, 4, P], F32, name="yT")
+            nc.tensor.transpose(out=nw_ps[:, 0, :], in_=nw_f[:], identity=ident[:])
+            nc.vector.tensor_copy(out=w4[:], in_=nw_ps[:, 0, 0:8])
 
-        rstd = {}
-        otile = {}
+        def regroup_weights(c):
+            wr = wraw[:].rearrange("p (c t) n -> p c t n", t=4)
+            nc.vector.tensor_copy(out=w_g[:, c, 0:384, :], in_=wr[:, c].rearrange("p t n -> p n t"))
 
-        def stats(g):
-            ss = small.tile([P, GROUP], F32, name="ss")
-            for jj in range(GROUP):
-                junk = junkp.tile([P, D], BF16, name="junk")
-                nc.scalar.activation(
-                    out=junk[:], in_=xg[g][:, jj, :], func=ACT.Square, accum_out=ss[:, jj : jj + 1]
-                )
-            sd = small.tile([P, GROUP], F32, name="sd")
-            nc.scalar.activation(out=sd[:], in_=ss[:], func=ACT.Sqrt, scale=1.0 / D, bias=eps_t[:, 0:1])
-            r = small.tile([P, GROUP], F32, name="rstd")
-            nc.vector.reciprocal(out=r[:], in_=sd[:])
-            rstd[g] = r
-
-        def bunch(bn):
-            g, half = divmod(bn, GROUP // BUNCH)
-            grp = gpool.tile([P, BUNCH * 2 * 512], BF16, name="grp", align_bytes=64)
-            for i in range(BUNCH):
-                jj = half * BUNCH + i
-                y = ypool.tile([P, D], F32, name="y")
-                nc.gpsimd.tensor_scalar(
-                    out=y[:],
-                    in0=xg[g][:, jj, :],
-                    scalar1=rstd[g][:, jj : jj + 1],
-                    scalar2=0.0,
-                    op0=ALU.mult,
-                    op1=ALU.add,
-                )
-                for c in range(2):
-                    yT = ps_t.tile([P, 4, P], F32, name="yT")
-                    for t in range(4):
-                        k0 = (c * 4 + t) * P
-                        nc.tensor.transpose(out=yT[:, t, :], in_=y[:, k0 : k0 + P], identity=ident[:])
-                    col = (i * 2 + c) * 512
-                    nc.vector.tensor_tensor(
-                        out=grp[:, col : col + 512].rearrange("p (k t) -> p k t", t=4),
-                        in0=yT[:].rearrange("p t k -> p k t"),
-                        in1=w4[:, c * 4 : (c + 1) * 4].unsqueeze(1).to_broadcast([P, P, 4]),
-                        op=ALU.mult,
-                    )
-            codes = gpool.tile([P, BUNCH * 2 * P], U32, name="codes", align_bytes=64)
-            scl = gpool.tile([P, BUNCH * 2 * P], U8, name="scl", align_bytes=64)
-            nc.vector.quantize_mx(out=codes[:].bitcast(FP8X4), scales=scl[:], in_=grp[:])
-
-            qk = ps_o.tile([P, BUNCH, 256], F32, name="qk")
-            vp = ps_o.tile([P, BUNCH, P], F32, name="vp")
-            for i in range(BUNCH):
-                for dst, wc, ws, n in ((qk, wqk_c, wqk_s, 256), (vp, wv_c, wv_s, P)):
-                    for c in range(2):
-                        col = (i * 2 + c) * P
-                        nc.tensor.matmul_mx(
-                            out=dst[:, i, :],
-                            lhsT=codes[:, col : col + P].bitcast(FP8X4),
-                            lhsT_scale=scl[:, col : col + P],
-                            rhs=wc[:, c * n : (c + 1) * n].bitcast(FP8X4),
-                            rhs_scale=ws[:, c * n : (c + 1) * n],
-                            start=(c == 0),
-                            stop=(c == 1),
-                        )
-
-            if half == 0:
-                otile[g] = opool.tile([P, 6, GROUP, HD], F32, name="otile")
-            o = otile[g]
-            j0 = half * BUNCH
-            ssq = small.tile([P, BUNCH * 4], F32, name="ssq")
-            for i in range(BUNCH):
-                for w in range(4):
-                    junk2 = junkp.tile([P, HD], BF16, name="junk2")
-                    nc.scalar.activation(
-                        out=junk2[:],
-                        in_=qk[:, i, w * HD : (w + 1) * HD],
-                        func=ACT.Square,
-                        accum_out=ssq[:, i * 4 + w : i * 4 + w + 1],
-                    )
-            nc.scalar.copy(
-                out=o[:, 4:6, j0 : j0 + BUNCH, :], in_=vp[:].rearrange("p i (w d) -> p w i d", d=HD)
+        def quant_weights():
+            nc.vector.quantize_mx(
+                out=w_c[:].bitcast(FP8X4), scales=w_s[:], in_=w_g[:].rearrange("p c n t -> p (c n t)")
             )
-            ssc = small.tile([P, BUNCH * 4], F32, name="ssc")
-            nc.vector.tensor_scalar_max(out=ssc[:], in0=ssq[:], scalar1=1e-24)
-            nrm = small.tile([P, BUNCH * 4], F32, name="nrm")
-            nc.scalar.activation(out=nrm[:], in_=ssc[:], func=ACT.Sqrt)
-            rn = small.tile([P, BUNCH * 4], F32, name="rn")
-            nc.vector.reciprocal(out=rn[:], in_=nrm[:])
+
+        def stat_cols(tau):
+            i = tau % 2
+            return (i, i + 1) if tau < 2 else (0, 2)
+
+        def sumsq(tau):
+            g, jj = divmod(tau, GROUP)
+            m, i = divmod(tau, 2)
+            if i == 0:
+                ss[m] = small.tile([P, 2], F32, name="ss")
+                sd[m] = small.tile([P, 2], F32, name="sd")
+                rstd[m] = small.tile([P, 2], F32, name="rstd")
+            junk = junkp.tile([P, D], BF16, name="junk")
+            nc.scalar.activation(
+                out=junk[:], in_=xg[g][:, jj, :], func=ACT.Square, accum_out=ss[m][:, i : i + 1]
+            )
+            if tau < 2 or i == 1:
+                lo, hi = stat_cols(tau)
+                nc.scalar.activation(
+                    out=sd[m][:, lo:hi], in_=ss[m][:, lo:hi], func=ACT.Sqrt, scale=1.0 / D, bias=eps_t[:, 0:1]
+                )
+
+        def rstd_recip(tau):
+            m, i = divmod(tau, 2)
+            if tau < 2 or i == 1:
+                lo, hi = stat_cols(tau)
+                nc.vector.reciprocal(out=rstd[m][:, lo:hi], in_=sd[m][:, lo:hi])
+
+        def ymul(tau):
+            g, jj = divmod(tau, GROUP)
+            m, i = divmod(tau, 2)
+            y = ypool.tile([P, D], F32, name="y")
+            ys[tau] = y
+            nc.gpsimd.tensor_scalar(
+                out=y[:],
+                in0=xg[g][:, jj, :],
+                scalar1=rstd[m][:, i : i + 1],
+                scalar2=0.0,
+                op0=ALU.mult,
+                op1=ALU.add,
+            )
+
+        def trans(tau):
+            for c in range(2):
+                yT = ps_t.tile([P, 4, P], F32, name="yT")
+                yts[(tau, c)] = yT
+                for t in range(4):
+                    k0 = (c * 4 + t) * P
+                    nc.tensor.transpose(out=yT[:, t, :], in_=ys[tau][:, k0 : k0 + P], identity=ident[:])
+
+        def evac(tau):
+            grp = gpool.tile([P, 1024], BF16, name="grp", align_bytes=64)
+            grps[tau] = grp
+            for c in range(2):
+                nc.vector.tensor_tensor(
+                    out=grp[:, c * 512 : (c + 1) * 512].rearrange("p (k t) -> p k t", t=4),
+                    in0=yts[(tau, c)][:].rearrange("p t k -> p k t"),
+                    in1=w4[:, c * 4 : (c + 1) * 4].unsqueeze(1).to_broadcast([P, P, 4]),
+                    op=ALU.mult,
+                )
+
+        def quant(tau):
+            codes = gpool.tile([P, 256], U32, name="codes", align_bytes=64)
+            scl = gpool.tile([P, 256], U8, name="scl", align_bytes=64)
+            cds[tau] = (codes, scl)
+            nc.vector.quantize_mx(out=codes[:].bitcast(FP8X4), scales=scl[:], in_=grps[tau][:])
+
+        def mx(tau):
+            po = ps_o.tile([P, 512], F32, name="po")
+            pos[tau] = po
+            codes, scl = cds[tau]
+            for c in range(2):
+                nc.tensor.matmul_mx(
+                    out=po[:],
+                    lhsT=codes[:, c * P : (c + 1) * P].bitcast(FP8X4),
+                    lhsT_scale=scl[:, c * P : (c + 1) * P],
+                    rhs=w_c[:, c * 512 : (c + 1) * 512].bitcast(FP8X4),
+                    rhs_scale=w_s[:, c * 512 : (c + 1) * 512],
+                    start=(c == 0),
+                    stop=(c == 1),
+                )
+
+        def heads(tau):
+            m, i = divmod(tau, 2)
+            g, jj = divmod(tau, GROUP)
+            if i == 0:
+                ssqs[m] = small.tile([P, 8], F32, name="ssq")
+            if jj == 0:
+                otile[g] = opool.tile([P, 6, GROUP, HD], F32, name="otile")
+            for w in range(4):
+                junk2 = junkp.tile([P, HD], BF16, name="junk2")
+                nc.scalar.activation(
+                    out=junk2[:],
+                    in_=pos[tau][:, w * HD : (w + 1) * HD],
+                    func=ACT.Square,
+                    accum_out=ssqs[m][:, i * 4 + w : i * 4 + w + 1],
+                )
+            nc.scalar.copy(
+                out=otile[g][:, 4:6, jj, :], in_=pos[tau][:, 256:384].rearrange("p (w d) -> p w d", d=HD)
+            )
+
+        nrm_in, nrm_out = {}, {}
+
+        def root(m):
+            nrm_in[m] = small.tile([P, 8], F32, name="ssc")
+            nc.scalar.activation(out=nrm_in[m][:], in_=ssqs[m][:], func=ACT.Relu, bias=tiny_n[:, 0:1])
+            nrm_out[m] = small.tile([P, 8], F32, name="nrm")
+            nc.scalar.activation(out=nrm_out[m][:], in_=nrm_in[m][:], func=ACT.Sqrt, bias=tiny_p[:, 0:1])
+
+        def recip(m):
+            rns[m] = small.tile([P, 8], F32, name="rn")
+            nc.vector.reciprocal(out=rns[m][:], in_=nrm_out[m][:])
+
+        def scale(tau):
+            m, i = divmod(tau, 2)
+            g, jj = divmod(tau, GROUP)
             nc.vector.tensor_tensor(
-                out=o[:, 0:4, j0 : j0 + BUNCH, :],
-                in0=qk[:].rearrange("p i (w d) -> p w i d", d=HD),
-                in1=rn[:].rearrange("p (i w) -> p w i", w=4).unsqueeze(3).to_broadcast([P, 4, BUNCH, HD]),
+                out=otile[g][:, 0:4, jj, :],
+                in0=pos[tau][:, 0:256].rearrange("p (w d) -> p w d", d=HD),
+                in1=rns[m][:, i * 4 : (i + 1) * 4].unsqueeze(2).to_broadcast([P, 4, HD]),
                 op=ALU.mult,
             )
 
@@ -191,10 +226,39 @@ def tile_sharedglobalattention_pa_t_kernel(tc, x, norm_w, Wq, Wk, Wv, out_0, out
                     out=ov[m][b][:, :, j0 : j0 + GROUP, :], in_=otile[g][:, 2 * m : 2 * m + 2, :, :]
                 )
 
-        for g in range(N_GROUPS):
-            if g + 1 < N_GROUPS:
-                load(g + 1)
-            stats(g)
-            for half in range(GROUP // BUNCH):
-                bunch(g * (GROUP // BUNCH) + half)
-            store(g)
+        def ok(tau):
+            return 0 <= tau < N_TILES
+
+        for n in range(-LOAD_LEAD, N_TILES + 5):
+            if (n + LOAD_LEAD) % GROUP == 0 and 0 < (n + LOAD_LEAD) // GROUP < N_GROUPS:
+                load((n + LOAD_LEAD) // GROUP)
+            if n == -SUMSQ_LEAD:
+                prep_norm_w()
+            if ok(n + Y_LEAD):
+                ymul(n + Y_LEAD)
+            if ok(n + 1):
+                trans(n + 1)
+            if ok(n - 1):
+                mx(n - 1)
+            if ok(n - 2):
+                heads(n - 2)
+                if (n - 2) % 2 == 1:
+                    root((n - 2) // 2)
+            if ok(n + SUMSQ_LEAD):
+                sumsq(n + SUMSQ_LEAD)
+            if ok(n):
+                evac(n)
+            if n == 0:
+                quant_weights()
+            if ok(n - 4):
+                if (n - 4) % 2 == 0:
+                    recip((n - 4) // 2)
+                scale(n - 4)
+            if ok(n):
+                quant(n)
+            if ok(n + SUMSQ_LEAD - 1):
+                rstd_recip(n + SUMSQ_LEAD - 1)
+            if n + SUMSQ_LEAD - 1 in (0, 1):
+                regroup_weights(n + SUMSQ_LEAD - 1)
+            if ok(n - 4) and (n - 4) % GROUP == GROUP - 1:
+                store((n - 4) // GROUP)

@@ -20,9 +20,10 @@ N_TILES = B * J
 N_GROUPS = N_TILES // GROUP
 FLOPS = 2 * B * L * D * 384
 
-LOAD_LEAD = 10
-SUMSQ_LEAD = 6
+LOAD_LEAD = 11
+SUMSQ_LEAD = 7
 Y_LEAD = 3
+G_COLS = 768
 
 
 def tile_sharedglobalattention_pa_t_kernel(tc, x, norm_w, Wq, Wk, Wv, out_0, out_1, out_2):
@@ -45,6 +46,8 @@ def tile_sharedglobalattention_pa_t_kernel(tc, x, norm_w, Wq, Wk, Wv, out_0, out
 
         xg, ss, sd, rstd, ys, yts, grps, cds, pos, ssqs, rns, otile = {}, {}, {}, {}, {}, {}, {}, {}, {}, {}, {}, {}
 
+        nw8 = const.tile([8, P], BF16, name="nw8")
+
         def load(g):
             b, j0 = divmod(g * GROUP, J)
             t = xpool.tile([P, GROUP, D], BF16, name="xg")
@@ -52,19 +55,20 @@ def tile_sharedglobalattention_pa_t_kernel(tc, x, norm_w, Wq, Wk, Wv, out_0, out
             if g == 0:
                 for jj in range(GROUP):
                     nc.sync.dma_start(out=t[:, jj : jj + 1, :], in_=xv[b][:, j0 + jj : j0 + jj + 1, :])
+                    if jj == 0:
+                        nc.sync.dma_start(out=nw8[:], in_=norm_w.rearrange("(c p) -> c p", p=P))
             else:
                 nc.sync.dma_start(out=t[:], in_=xv[b][:, j0 : j0 + GROUP, :])
 
         load(0)
 
-        nw_rows = const.tile([P, P], BF16, name="nw_rows")
-        nc.gpsimd.memset(nw_rows[:], 0.0)
         wraw = const.tile([P, 8, 384], BF16, name="wraw")
         for m, w in enumerate((Wq, Wk, Wv)):
             nc.scalar.dma_start(
                 out=wraw[:, :, m * P : (m + 1) * P], in_=w.rearrange("(c p) n -> p c n", p=P)
             )
-        nc.scalar.dma_start(out=nw_rows[0:8, :], in_=norm_w.rearrange("(c p) -> c p", p=P))
+        nw_f = const.tile([P, P], F32, name="nw_f")
+        nc.vector.memset(nw_f[:], 0.0)
         eps_t = const.tile([P, 1], F32, name="eps_t")
         nc.vector.memset(eps_t[:], 1e-6)
         tiny_p = const.tile([P, 1], F32, name="tiny_p")
@@ -82,8 +86,7 @@ def tile_sharedglobalattention_pa_t_kernel(tc, x, norm_w, Wq, Wk, Wv, out_0, out
         w4 = const.tile([P, 8], F32, name="w4")
 
         def prep_norm_w():
-            nw_f = const.tile([P, P], F32, name="nw_f")
-            nc.vector.tensor_copy(out=nw_f[:], in_=nw_rows[:])
+            nc.vector.tensor_copy(out=nw_f[0:8, :], in_=nw8[:])
             nw_ps = ps_t.tile([P, 4, P], F32, name="yT")
             nc.tensor.transpose(out=nw_ps[:, 0, :], in_=nw_f[:], identity=ident[:])
             nc.vector.tensor_copy(out=w4[:], in_=nw_ps[:, 0, 0:8])
@@ -112,6 +115,9 @@ def tile_sharedglobalattention_pa_t_kernel(tc, x, norm_w, Wq, Wk, Wv, out_0, out
             nc.scalar.activation(
                 out=junk[:], in_=xg[g][:, jj, :], func=ACT.Square, accum_out=ss[m][:, i : i + 1]
             )
+
+        def rms(tau):
+            m, i = divmod(tau, 2)
             if tau < 2 or i == 1:
                 lo, hi = stat_cols(tau)
                 nc.scalar.activation(
@@ -130,12 +136,23 @@ def tile_sharedglobalattention_pa_t_kernel(tc, x, norm_w, Wq, Wk, Wv, out_0, out
             y = ypool.tile([P, D], F32, name="y")
             ys[tau] = y
             nc.gpsimd.tensor_scalar(
-                out=y[:],
-                in0=xg[g][:, jj, :],
+                out=y[:, 0:G_COLS],
+                in0=xg[g][:, jj, 0:G_COLS],
                 scalar1=rstd[m][:, i : i + 1],
                 scalar2=0.0,
                 op0=ALU.mult,
                 op1=ALU.add,
+            )
+
+        def ymul_v(tau):
+            g, jj = divmod(tau, GROUP)
+            m, i = divmod(tau, 2)
+            nc.vector.tensor_scalar(
+                out=ys[tau][:, G_COLS:D],
+                in0=xg[g][:, jj, G_COLS:D],
+                scalar1=rstd[m][:, i : i + 1],
+                scalar2=None,
+                op0=ALU.mult,
             )
 
         def trans(tau):
@@ -199,9 +216,11 @@ def tile_sharedglobalattention_pa_t_kernel(tc, x, norm_w, Wq, Wk, Wv, out_0, out
 
         nrm_in, nrm_out = {}, {}
 
-        def root(m):
+        def clamp(m):
             nrm_in[m] = small.tile([P, 8], F32, name="ssc")
             nc.scalar.activation(out=nrm_in[m][:], in_=ssqs[m][:], func=ACT.Relu, bias=tiny_n[:, 0:1])
+
+        def root(m):
             nrm_out[m] = small.tile([P, 8], F32, name="nrm")
             nc.scalar.activation(out=nrm_out[m][:], in_=nrm_in[m][:], func=ACT.Sqrt, bias=tiny_p[:, 0:1])
 
@@ -240,25 +259,32 @@ def tile_sharedglobalattention_pa_t_kernel(tc, x, norm_w, Wq, Wk, Wv, out_0, out
                 trans(n + 1)
             if ok(n - 1):
                 mx(n - 1)
+            pair_done = ok(n - 2) and (n - 2) % 2 == 1
             if ok(n - 2):
                 heads(n - 2)
-                if (n - 2) % 2 == 1:
-                    root((n - 2) // 2)
+            if pair_done:
+                clamp((n - 2) // 2)
+            if ok(n + SUMSQ_LEAD - 1):
+                rms(n + SUMSQ_LEAD - 1)
             if ok(n + SUMSQ_LEAD):
                 sumsq(n + SUMSQ_LEAD)
+            if pair_done:
+                root((n - 2) // 2)
+            if ok(n - 4) and (n - 4) % 2 == 0:
+                recip((n - 4) // 2)
             if ok(n):
                 evac(n)
             if n == 0:
                 quant_weights()
             if ok(n - 4):
-                if (n - 4) % 2 == 0:
-                    recip((n - 4) // 2)
                 scale(n - 4)
             if ok(n):
                 quant(n)
-            if ok(n + SUMSQ_LEAD - 1):
-                rstd_recip(n + SUMSQ_LEAD - 1)
-            if n + SUMSQ_LEAD - 1 in (0, 1):
-                regroup_weights(n + SUMSQ_LEAD - 1)
+            if ok(n + Y_LEAD):
+                ymul_v(n + Y_LEAD)
+            if ok(n + SUMSQ_LEAD - 2):
+                rstd_recip(n + SUMSQ_LEAD - 2)
+            if n + SUMSQ_LEAD - 2 in (0, 1):
+                regroup_weights(n + SUMSQ_LEAD - 2)
             if ok(n - 4) and (n - 4) % GROUP == GROUP - 1:
                 store((n - 4) // GROUP)

@@ -23,7 +23,7 @@ FLOPS = 2 * B * L * D * 384
 LOAD_LEAD = 11
 SUMSQ_LEAD = 7
 Y_LEAD = 3
-G_COLS = 768
+G_COLS = 640
 
 
 def tile_sharedglobalattention_pa_t_kernel(tc, x, norm_w, Wq, Wk, Wv, out_0, out_1, out_2):
@@ -44,7 +44,7 @@ def tile_sharedglobalattention_pa_t_kernel(tc, x, norm_w, Wq, Wk, Wv, out_0, out
         outs = (out_0, out_1, out_2)
         ov = [[o[b].rearrange("n (p j) d -> p n j d", j=J) for b in range(B)] for o in outs]
 
-        xg, ss, sd, rstd, ys, yts, grps, cds, pos, ssqs, rns, otile = {}, {}, {}, {}, {}, {}, {}, {}, {}, {}, {}, {}
+        xg, ss, rstd, ys, yts, grps, cds, pos, ssqs, rns, otile = {}, {}, {}, {}, {}, {}, {}, {}, {}, {}, {}
 
         nw8 = const.tile([8, P], BF16, name="nw8")
 
@@ -76,7 +76,7 @@ def tile_sharedglobalattention_pa_t_kernel(tc, x, norm_w, Wq, Wk, Wv, out_0, out
         tiny_n = const.tile([P, 1], F32, name="tiny_n")
         nc.vector.memset(tiny_n[:], -1e-24)
         warm = const.tile([P, 1], F32, name="warm")
-        nc.scalar.activation(out=warm[:], in_=eps_t[:], func=ACT.Sqrt)
+        nc.scalar.activation(out=warm[:], in_=eps_t[:], func=ACT.Abs_reciprocal_sqrt)
         ident = const.tile([P, P], F32, name="ident")
         make_identity(nc, ident[:])
         w_g = const.tile([P, 2, 512, 4], BF16, name="w_g", align_bytes=64)
@@ -109,7 +109,6 @@ def tile_sharedglobalattention_pa_t_kernel(tc, x, norm_w, Wq, Wk, Wv, out_0, out
             m, i = divmod(tau, 2)
             if i == 0:
                 ss[m] = small.tile([P, 2], F32, name="ss")
-                sd[m] = small.tile([P, 2], F32, name="sd")
                 rstd[m] = small.tile([P, 2], F32, name="rstd")
             junk = junkp.tile([P, D], BF16, name="junk")
             nc.scalar.activation(
@@ -121,14 +120,12 @@ def tile_sharedglobalattention_pa_t_kernel(tc, x, norm_w, Wq, Wk, Wv, out_0, out
             if tau < 2 or i == 1:
                 lo, hi = stat_cols(tau)
                 nc.scalar.activation(
-                    out=sd[m][:, lo:hi], in_=ss[m][:, lo:hi], func=ACT.Sqrt, scale=1.0 / D, bias=eps_t[:, 0:1]
+                    out=rstd[m][:, lo:hi],
+                    in_=ss[m][:, lo:hi],
+                    func=ACT.Abs_reciprocal_sqrt,
+                    scale=1.0 / D,
+                    bias=eps_t[:, 0:1],
                 )
-
-        def rstd_recip(tau):
-            m, i = divmod(tau, 2)
-            if tau < 2 or i == 1:
-                lo, hi = stat_cols(tau)
-                nc.vector.reciprocal(out=rstd[m][:, lo:hi], in_=sd[m][:, lo:hi])
 
         def ymul(tau):
             g, jj = divmod(tau, GROUP)
@@ -214,19 +211,17 @@ def tile_sharedglobalattention_pa_t_kernel(tc, x, norm_w, Wq, Wk, Wv, out_0, out
                 out=otile[g][:, 4:6, jj, :], in_=pos[tau][:, 256:384].rearrange("p (w d) -> p w d", d=HD)
             )
 
-        nrm_in, nrm_out = {}, {}
+        nrm_in = {}
 
         def clamp(m):
             nrm_in[m] = small.tile([P, 8], F32, name="ssc")
             nc.scalar.activation(out=nrm_in[m][:], in_=ssqs[m][:], func=ACT.Relu, bias=tiny_n[:, 0:1])
 
         def root(m):
-            nrm_out[m] = small.tile([P, 8], F32, name="nrm")
-            nc.scalar.activation(out=nrm_out[m][:], in_=nrm_in[m][:], func=ACT.Sqrt, bias=tiny_p[:, 0:1])
-
-        def recip(m):
             rns[m] = small.tile([P, 8], F32, name="rn")
-            nc.vector.reciprocal(out=rns[m][:], in_=nrm_out[m][:])
+            nc.scalar.activation(
+                out=rns[m][:], in_=nrm_in[m][:], func=ACT.Abs_reciprocal_sqrt, bias=tiny_p[:, 0:1]
+            )
 
         def scale(tau):
             m, i = divmod(tau, 2)
@@ -270,8 +265,6 @@ def tile_sharedglobalattention_pa_t_kernel(tc, x, norm_w, Wq, Wk, Wv, out_0, out
                 sumsq(n + SUMSQ_LEAD)
             if pair_done:
                 root((n - 2) // 2)
-            if ok(n - 4) and (n - 4) % 2 == 0:
-                recip((n - 4) // 2)
             if ok(n):
                 evac(n)
             if n == 0:
@@ -282,8 +275,6 @@ def tile_sharedglobalattention_pa_t_kernel(tc, x, norm_w, Wq, Wk, Wv, out_0, out
                 quant(n)
             if ok(n + Y_LEAD):
                 ymul_v(n + Y_LEAD)
-            if ok(n + SUMSQ_LEAD - 2):
-                rstd_recip(n + SUMSQ_LEAD - 2)
             if n + SUMSQ_LEAD - 2 in (0, 1):
                 regroup_weights(n + SUMSQ_LEAD - 2)
             if ok(n - 4) and (n - 4) % GROUP == GROUP - 1:

@@ -23,7 +23,7 @@ FLOPS = 2 * B * L * D * 384
 LOAD_LEAD = 11
 SUMSQ_LEAD = 7
 Y_LEAD = 3
-G_COLS = 640
+G_COLS = 768
 
 
 def tile_sharedglobalattention_pa_t_kernel(tc, x, norm_w, Wq, Wk, Wv, out_0, out_1, out_2):
@@ -207,9 +207,6 @@ def tile_sharedglobalattention_pa_t_kernel(tc, x, norm_w, Wq, Wk, Wv, out_0, out
                     func=ACT.Square,
                     accum_out=ssqs[m][:, i * 4 + w : i * 4 + w + 1],
                 )
-            nc.scalar.copy(
-                out=otile[g][:, 4:6, jj, :], in_=pos[tau][:, 256:384].rearrange("p (w d) -> p w d", d=HD)
-            )
 
         nrm_in = {}
 
@@ -231,6 +228,9 @@ def tile_sharedglobalattention_pa_t_kernel(tc, x, norm_w, Wq, Wk, Wv, out_0, out
                 in0=pos[tau][:, 0:256].rearrange("p (w d) -> p w d", d=HD),
                 in1=rns[m][:, i * 4 : (i + 1) * 4].unsqueeze(2).to_broadcast([P, 4, HD]),
                 op=ALU.mult,
+            )
+            nc.vector.tensor_copy(
+                out=otile[g][:, 4:6, jj, :], in_=pos[tau][:, 256:384].rearrange("p (w d) -> p w d", d=HD)
             )
 
         def store(g):

@@ -23,7 +23,7 @@ FLOPS = 2 * B * L * D * 384
 LOAD_LEAD = 11
 SUMSQ_LEAD = 7
 Y_LEAD = 3
-G_COLS = 768
+G_COLS_ODD = 384
 
 
 def tile_sharedglobalattention_pa_t_kernel(tc, x, norm_w, Wq, Wk, Wv, out_0, out_1, out_2):
@@ -132,9 +132,10 @@ def tile_sharedglobalattention_pa_t_kernel(tc, x, norm_w, Wq, Wk, Wv, out_0, out
             m, i = divmod(tau, 2)
             y = ypool.tile([P, D], F32, name="y")
             ys[tau] = y
+            cols = D if i == 0 else G_COLS_ODD
             nc.gpsimd.tensor_scalar(
-                out=y[:, 0:G_COLS],
-                in0=xg[g][:, jj, 0:G_COLS],
+                out=y[:, 0:cols],
+                in0=xg[g][:, jj, 0:cols],
                 scalar1=rstd[m][:, i : i + 1],
                 scalar2=0.0,
                 op0=ALU.mult,
@@ -145,8 +146,8 @@ def tile_sharedglobalattention_pa_t_kernel(tc, x, norm_w, Wq, Wk, Wv, out_0, out
             g, jj = divmod(tau, GROUP)
             m, i = divmod(tau, 2)
             nc.vector.tensor_scalar(
-                out=ys[tau][:, G_COLS:D],
-                in0=xg[g][:, jj, G_COLS:D],
+                out=ys[tau][:, G_COLS_ODD:D],
+                in0=xg[g][:, jj, G_COLS_ODD:D],
                 scalar1=rstd[m][:, i : i + 1],
                 scalar2=None,
                 op0=ALU.mult,
@@ -161,31 +162,35 @@ def tile_sharedglobalattention_pa_t_kernel(tc, x, norm_w, Wq, Wk, Wv, out_0, out
                     nc.tensor.transpose(out=yT[:, t, :], in_=ys[tau][:, k0 : k0 + P], identity=ident[:])
 
         def evac(tau):
-            grp = gpool.tile([P, 1024], BF16, name="grp", align_bytes=64)
-            grps[tau] = grp
+            m, i = divmod(tau, 2)
+            if i == 0:
+                grps[m] = gpool.tile([P, 2048], BF16, name="grp", align_bytes=64)
             for c in range(2):
+                col = (i * 2 + c) * 512
                 nc.vector.tensor_tensor(
-                    out=grp[:, c * 512 : (c + 1) * 512].rearrange("p (k t) -> p k t", t=4),
+                    out=grps[m][:, col : col + 512].rearrange("p (k t) -> p k t", t=4),
                     in0=yts[(tau, c)][:].rearrange("p t k -> p k t"),
                     in1=w4[:, c * 4 : (c + 1) * 4].unsqueeze(1).to_broadcast([P, P, 4]),
                     op=ALU.mult,
                 )
 
-        def quant(tau):
-            codes = gpool.tile([P, 256], U32, name="codes", align_bytes=64)
-            scl = gpool.tile([P, 256], U8, name="scl", align_bytes=64)
-            cds[tau] = (codes, scl)
-            nc.vector.quantize_mx(out=codes[:].bitcast(FP8X4), scales=scl[:], in_=grps[tau][:])
+        def quant(m):
+            codes = gpool.tile([P, 512], U32, name="codes", align_bytes=64)
+            scl = gpool.tile([P, 512], U8, name="scl", align_bytes=64)
+            cds[m] = (codes, scl)
+            nc.vector.quantize_mx(out=codes[:].bitcast(FP8X4), scales=scl[:], in_=grps[m][:])
 
         def mx(tau):
             po = ps_o.tile([P, 512], F32, name="po")
             pos[tau] = po
-            codes, scl = cds[tau]
+            m, i = divmod(tau, 2)
+            codes, scl = cds[m]
             for c in range(2):
+                col = (i * 2 + c) * P
                 nc.tensor.matmul_mx(
                     out=po[:],
-                    lhsT=codes[:, c * P : (c + 1) * P].bitcast(FP8X4),
-                    lhsT_scale=scl[:, c * P : (c + 1) * P],
+                    lhsT=codes[:, col : col + P].bitcast(FP8X4),
+                    lhsT_scale=scl[:, col : col + P],
                     rhs=w_c[:, c * 512 : (c + 1) * 512].bitcast(FP8X4),
                     rhs_scale=w_s[:, c * 512 : (c + 1) * 512],
                     start=(c == 0),
@@ -207,6 +212,9 @@ def tile_sharedglobalattention_pa_t_kernel(tc, x, norm_w, Wq, Wk, Wv, out_0, out
                     func=ACT.Square,
                     accum_out=ssqs[m][:, i * 4 + w : i * 4 + w + 1],
                 )
+            nc.scalar.copy(
+                out=otile[g][:, 4:6, jj, :], in_=pos[tau][:, 256:384].rearrange("p (w d) -> p w d", d=HD)
+            )
 
         nrm_in = {}
 
@@ -229,9 +237,6 @@ def tile_sharedglobalattention_pa_t_kernel(tc, x, norm_w, Wq, Wk, Wv, out_0, out
                 in1=rns[m][:, i * 4 : (i + 1) * 4].unsqueeze(2).to_broadcast([P, 4, HD]),
                 op=ALU.mult,
             )
-            nc.vector.tensor_copy(
-                out=otile[g][:, 4:6, jj, :], in_=pos[tau][:, 256:384].rearrange("p (w d) -> p w d", d=HD)
-            )
 
         def store(g):
             b, j0 = divmod(g * GROUP, J)
@@ -243,7 +248,7 @@ def tile_sharedglobalattention_pa_t_kernel(tc, x, norm_w, Wq, Wk, Wv, out_0, out
         def ok(tau):
             return 0 <= tau < N_TILES
 
-        for n in range(-LOAD_LEAD, N_TILES + 5):
+        for n in range(-LOAD_LEAD, N_TILES + 6):
             if (n + LOAD_LEAD) % GROUP == 0 and 0 < (n + LOAD_LEAD) // GROUP < N_GROUPS:
                 load((n + LOAD_LEAD) // GROUP)
             if n == -SUMSQ_LEAD:
@@ -252,30 +257,30 @@ def tile_sharedglobalattention_pa_t_kernel(tc, x, norm_w, Wq, Wk, Wv, out_0, out
                 ymul(n + Y_LEAD)
             if ok(n + 1):
                 trans(n + 1)
-            if ok(n - 1):
-                mx(n - 1)
-            pair_done = ok(n - 2) and (n - 2) % 2 == 1
             if ok(n - 2):
-                heads(n - 2)
+                mx(n - 2)
+            pair_done = ok(n - 3) and (n - 3) % 2 == 1
+            if ok(n - 3):
+                heads(n - 3)
             if pair_done:
-                clamp((n - 2) // 2)
+                clamp((n - 3) // 2)
             if ok(n + SUMSQ_LEAD - 1):
                 rms(n + SUMSQ_LEAD - 1)
             if ok(n + SUMSQ_LEAD):
                 sumsq(n + SUMSQ_LEAD)
             if pair_done:
-                root((n - 2) // 2)
+                root((n - 3) // 2)
             if ok(n):
                 evac(n)
             if n == 0:
                 quant_weights()
-            if ok(n - 4):
-                scale(n - 4)
-            if ok(n):
-                quant(n)
-            if ok(n + Y_LEAD):
+            if ok(n - 5):
+                scale(n - 5)
+            if ok(n) and n % 2 == 1:
+                quant(n // 2)
+            if ok(n + Y_LEAD) and (n + Y_LEAD) % 2 == 1:
                 ymul_v(n + Y_LEAD)
             if n + SUMSQ_LEAD - 2 in (0, 1):
                 regroup_weights(n + SUMSQ_LEAD - 2)
-            if ok(n - 4) and (n - 4) % GROUP == GROUP - 1:
-                store((n - 4) // GROUP)
+            if ok(n - 5) and (n - 5) % GROUP == GROUP - 1:
+                store((n - 5) // GROUP)

@@ -23,7 +23,7 @@ FLOPS = 2 * B * L * D * 384
 LOAD_LEAD = 11
 SUMSQ_LEAD = 7
 Y_LEAD = 3
-G_COLS_ODD = 384
+G_COLS = 704
 
 
 def tile_sharedglobalattention_pa_t_kernel(tc, x, norm_w, Wq, Wk, Wv, out_0, out_1, out_2):
@@ -132,22 +132,23 @@ def tile_sharedglobalattention_pa_t_kernel(tc, x, norm_w, Wq, Wk, Wv, out_0, out
             m, i = divmod(tau, 2)
             y = ypool.tile([P, D], F32, name="y")
             ys[tau] = y
-            cols = D if i == 0 else G_COLS_ODD
-            nc.gpsimd.tensor_scalar(
-                out=y[:, 0:cols],
-                in0=xg[g][:, jj, 0:cols],
-                scalar1=rstd[m][:, i : i + 1],
-                scalar2=0.0,
-                op0=ALU.mult,
-                op1=ALU.add,
-            )
+            if tau > 0:
+                nc.gpsimd.tensor_scalar(
+                    out=y[:, 0:G_COLS],
+                    in0=xg[g][:, jj, 0:G_COLS],
+                    scalar1=rstd[m][:, i : i + 1],
+                    scalar2=0.0,
+                    op0=ALU.mult,
+                    op1=ALU.add,
+                )
 
         def ymul_v(tau):
             g, jj = divmod(tau, GROUP)
             m, i = divmod(tau, 2)
+            lo = G_COLS if tau > 0 else 0
             nc.vector.tensor_scalar(
-                out=ys[tau][:, G_COLS_ODD:D],
-                in0=xg[g][:, jj, G_COLS_ODD:D],
+                out=ys[tau][:, lo:D],
+                in0=xg[g][:, jj, lo:D],
                 scalar1=rstd[m][:, i : i + 1],
                 scalar2=None,
                 op0=ALU.mult,
@@ -162,35 +163,31 @@ def tile_sharedglobalattention_pa_t_kernel(tc, x, norm_w, Wq, Wk, Wv, out_0, out
                     nc.tensor.transpose(out=yT[:, t, :], in_=ys[tau][:, k0 : k0 + P], identity=ident[:])
 
         def evac(tau):
-            m, i = divmod(tau, 2)
-            if i == 0:
-                grps[m] = gpool.tile([P, 2048], BF16, name="grp", align_bytes=64)
+            grp = gpool.tile([P, 1024], BF16, name="grp", align_bytes=64)
+            grps[tau] = grp
             for c in range(2):
-                col = (i * 2 + c) * 512
                 nc.vector.tensor_tensor(
-                    out=grps[m][:, col : col + 512].rearrange("p (k t) -> p k t", t=4),
+                    out=grp[:, c * 512 : (c + 1) * 512].rearrange("p (k t) -> p k t", t=4),
                     in0=yts[(tau, c)][:].rearrange("p t k -> p k t"),
                     in1=w4[:, c * 4 : (c + 1) * 4].unsqueeze(1).to_broadcast([P, P, 4]),
                     op=ALU.mult,
                 )
 
-        def quant(m):
-            codes = gpool.tile([P, 512], U32, name="codes", align_bytes=64)
-            scl = gpool.tile([P, 512], U8, name="scl", align_bytes=64)
-            cds[m] = (codes, scl)
-            nc.vector.quantize_mx(out=codes[:].bitcast(FP8X4), scales=scl[:], in_=grps[m][:])
+        def quant(tau):
+            codes = gpool.tile([P, 256], U32, name="codes", align_bytes=64)
+            scl = gpool.tile([P, 256], U8, name="scl", align_bytes=64)
+            cds[tau] = (codes, scl)
+            nc.vector.quantize_mx(out=codes[:].bitcast(FP8X4), scales=scl[:], in_=grps[tau][:])
 
         def mx(tau):
             po = ps_o.tile([P, 512], F32, name="po")
             pos[tau] = po
-            m, i = divmod(tau, 2)
-            codes, scl = cds[m]
+            codes, scl = cds[tau]
             for c in range(2):
-                col = (i * 2 + c) * P
                 nc.tensor.matmul_mx(
                     out=po[:],
-                    lhsT=codes[:, col : col + P].bitcast(FP8X4),
-                    lhsT_scale=scl[:, col : col + P],
+                    lhsT=codes[:, c * P : (c + 1) * P].bitcast(FP8X4),
+                    lhsT_scale=scl[:, c * P : (c + 1) * P],
                     rhs=w_c[:, c * 512 : (c + 1) * 512].bitcast(FP8X4),
                     rhs_scale=w_s[:, c * 512 : (c + 1) * 512],
                     start=(c == 0),
@@ -238,17 +235,17 @@ def tile_sharedglobalattention_pa_t_kernel(tc, x, norm_w, Wq, Wk, Wv, out_0, out
                 op=ALU.mult,
             )
 
-        def store(g):
+        def store(g, lo, hi):
             b, j0 = divmod(g * GROUP, J)
             for m in range(3):
                 nc.sync.dma_start(
-                    out=ov[m][b][:, :, j0 : j0 + GROUP, :], in_=otile[g][:, 2 * m : 2 * m + 2, :, :]
+                    out=ov[m][b][:, :, j0 + lo : j0 + hi, :], in_=otile[g][:, 2 * m : 2 * m + 2, lo:hi, :]
                 )
 
         def ok(tau):
             return 0 <= tau < N_TILES
 
-        for n in range(-LOAD_LEAD, N_TILES + 6):
+        for n in range(-LOAD_LEAD, N_TILES + 5):
             if (n + LOAD_LEAD) % GROUP == 0 and 0 < (n + LOAD_LEAD) // GROUP < N_GROUPS:
                 load((n + LOAD_LEAD) // GROUP)
             if n == -SUMSQ_LEAD:
@@ -257,30 +254,35 @@ def tile_sharedglobalattention_pa_t_kernel(tc, x, norm_w, Wq, Wk, Wv, out_0, out
                 ymul(n + Y_LEAD)
             if ok(n + 1):
                 trans(n + 1)
+            if ok(n - 1):
+                mx(n - 1)
+            pair_done = ok(n - 2) and (n - 2) % 2 == 1
             if ok(n - 2):
-                mx(n - 2)
-            pair_done = ok(n - 3) and (n - 3) % 2 == 1
-            if ok(n - 3):
-                heads(n - 3)
+                heads(n - 2)
             if pair_done:
-                clamp((n - 3) // 2)
+                clamp((n - 2) // 2)
             if ok(n + SUMSQ_LEAD - 1):
                 rms(n + SUMSQ_LEAD - 1)
             if ok(n + SUMSQ_LEAD):
                 sumsq(n + SUMSQ_LEAD)
             if pair_done:
-                root((n - 3) // 2)
+                root((n - 2) // 2)
             if ok(n):
                 evac(n)
             if n == 0:
                 quant_weights()
-            if ok(n - 5):
-                scale(n - 5)
-            if ok(n) and n % 2 == 1:
-                quant(n // 2)
-            if ok(n + Y_LEAD) and (n + Y_LEAD) % 2 == 1:
+            if ok(n - 4):
+                scale(n - 4)
+            if ok(n):
+                quant(n)
+            if ok(n + Y_LEAD):
                 ymul_v(n + Y_LEAD)
             if n + SUMSQ_LEAD - 2 in (0, 1):
                 regroup_weights(n + SUMSQ_LEAD - 2)
-            if ok(n - 5) and (n - 5) % GROUP == GROUP - 1:
-                store((n - 5) // GROUP)
+            if ok(n - 4):
+                g_out, j_out = divmod(n - 4, GROUP)
+                if g_out < N_GROUPS - 1:
+                    if j_out == GROUP - 1:
+                        store(g_out, 0, GROUP)
+                elif j_out % 2 == 1:
+                    store(g_out, j_out - 1, j_out + 1)

@@ -12,17 +12,27 @@ ACT = mybir.ActivationFunctionType
 ALU = mybir.AluOpType
 
 P = 128
+PACK = 4
 B, L, D = 4, 2048, 1024
 HD = 64
+N_QK = 256
+N_QKV = 384
+N_PASS = 512
+PASSES = D // (P * PACK)
+CHUNKS = D // P
 J = L // P
 GROUP = 4
 N_TILES = B * J
 N_GROUPS = N_TILES // GROUP
-FLOPS = 2 * B * L * D * 384
+FLOPS = 2 * B * L * D * N_QKV
 
 LOAD_LEAD = 11
 SUMSQ_LEAD = 7
 Y_LEAD = 3
+TRANSPOSE_LEAD = 1
+MX_LAG = 1
+HEAD_LAG = 2
+SCALE_LAG = 4
 G_COLS = 704
 
 
@@ -40,198 +50,200 @@ def tile_sharedglobalattention_pa_t_kernel(tc, x, norm_w, Wq, Wk, Wv, out_0, out
         ps_o = ctx.enter_context(tc.psum_pool(name="ps_o", bufs=4))
         ctx.enter_context(tc.manual_schedule())
 
-        xv = [x[b].rearrange("(p j) d -> p j d", j=J) for b in range(B)]
-        outs = (out_0, out_1, out_2)
-        ov = [[o[b].rearrange("n (p j) d -> p n j d", j=J) for b in range(B)] for o in outs]
+        x_rows = [x[b].rearrange("(p j) d -> p j d", j=J) for b in range(B)]
+        out_rows = [[o[b].rearrange("n (p j) d -> p n j d", j=J) for b in range(B)] for o in (out_0, out_1, out_2)]
 
-        xg, ss, rstd, ys, yts, grps, cds, pos, ssqs, rns, otile = {}, {}, {}, {}, {}, {}, {}, {}, {}, {}, {}
+        x_group, sumsq_pair, rrms_pair, y_tile, yT_bank, h_tile, h_mx = {}, {}, {}, {}, {}, {}, {}
+        qkv_tile, headsq_pair, clamped_pair, rnorm_pair, out_group = {}, {}, {}, {}, {}
 
-        nw8 = const.tile([8, P], BF16, name="nw8")
+        nw8 = const.tile([CHUNKS, P], BF16, name="nw8")
 
         def load(g):
             b, j0 = divmod(g * GROUP, J)
             t = xpool.tile([P, GROUP, D], BF16, name="xg")
-            xg[g] = t
+            x_group[g] = t
             if g == 0:
                 for jj in range(GROUP):
-                    nc.sync.dma_start(out=t[:, jj : jj + 1, :], in_=xv[b][:, j0 + jj : j0 + jj + 1, :])
+                    nc.sync.dma_start(out=t[:, jj : jj + 1, :], in_=x_rows[b][:, j0 + jj : j0 + jj + 1, :])
                     if jj == 0:
                         nc.sync.dma_start(out=nw8[:], in_=norm_w.rearrange("(c p) -> c p", p=P))
             else:
-                nc.sync.dma_start(out=t[:], in_=xv[b][:, j0 : j0 + GROUP, :])
+                nc.sync.dma_start(out=t[:], in_=x_rows[b][:, j0 : j0 + GROUP, :])
 
         load(0)
 
-        wraw = const.tile([P, 8, 384], BF16, name="wraw")
+        w_raw = const.tile([P, CHUNKS, N_QKV], BF16, name="wraw")
         for m, w in enumerate((Wq, Wk, Wv)):
             nc.scalar.dma_start(
-                out=wraw[:, :, m * P : (m + 1) * P], in_=w.rearrange("(c p) n -> p c n", p=P)
+                out=w_raw[:, :, m * P : (m + 1) * P], in_=w.rearrange("(c p) n -> p c n", p=P)
             )
-        nw_f = const.tile([P, P], F32, name="nw_f")
-        nc.vector.memset(nw_f[:], 0.0)
-        eps_t = const.tile([P, 1], F32, name="eps_t")
-        nc.vector.memset(eps_t[:], 1e-6)
-        tiny_p = const.tile([P, 1], F32, name="tiny_p")
-        nc.vector.memset(tiny_p[:], 1e-24)
-        tiny_n = const.tile([P, 1], F32, name="tiny_n")
-        nc.vector.memset(tiny_n[:], -1e-24)
+        nw_rows = const.tile([P, P], F32, name="nw_f")
+        nc.vector.memset(nw_rows[:], 0.0)
+        eps_rms = const.tile([P, 1], F32, name="eps_t")
+        nc.vector.memset(eps_rms[:], 1e-6)
+        eps_sq = const.tile([P, 1], F32, name="tiny_p")
+        nc.vector.memset(eps_sq[:], 1e-24)
+        minus_eps_sq = const.tile([P, 1], F32, name="tiny_n")
+        nc.vector.memset(minus_eps_sq[:], -1e-24)
         warm = const.tile([P, 1], F32, name="warm")
-        nc.scalar.activation(out=warm[:], in_=eps_t[:], func=ACT.Abs_reciprocal_sqrt)
+        nc.scalar.activation(out=warm[:], in_=eps_rms[:], func=ACT.Abs_reciprocal_sqrt)
         ident = const.tile([P, P], F32, name="ident")
         make_identity(nc, ident[:])
-        w_g = const.tile([P, 2, 512, 4], BF16, name="w_g", align_bytes=64)
-        nc.gpsimd.memset(w_g[:, :, 384:512, :], 0.0)
-        w_c = const.tile([P, 1024], U32, name="w_c", align_bytes=64)
-        w_s = const.tile([P, 1024], U8, name="w_s", align_bytes=64)
-        w4 = const.tile([P, 8], F32, name="w4")
+        w_grouped = const.tile([P, PASSES, N_PASS, PACK], BF16, name="w_g", align_bytes=64)
+        nc.gpsimd.memset(w_grouped[:, :, N_QKV:N_PASS, :], 0.0)
+        w_codes = const.tile([P, PASSES * N_PASS], U32, name="w_c", align_bytes=64)
+        w_scales = const.tile([P, PASSES * N_PASS], U8, name="w_s", align_bytes=64)
+        nw_kt = const.tile([P, CHUNKS], F32, name="w4")
 
-        def prep_norm_w():
-            nc.vector.tensor_copy(out=nw_f[0:8, :], in_=nw8[:])
-            nw_ps = ps_t.tile([P, 4, P], F32, name="yT")
-            nc.tensor.transpose(out=nw_ps[:, 0, :], in_=nw_f[:], identity=ident[:])
-            nc.vector.tensor_copy(out=w4[:], in_=nw_ps[:, 0, 0:8])
+        def spread_norm_w():
+            nc.vector.tensor_copy(out=nw_rows[0:CHUNKS, :], in_=nw8[:])
+            nw_ps = ps_t.tile([P, PACK, P], F32, name="yT")
+            nc.tensor.transpose(out=nw_ps[:, 0, :], in_=nw_rows[:], identity=ident[:])
+            nc.vector.tensor_copy(out=nw_kt[:], in_=nw_ps[:, 0, 0:CHUNKS])
 
         def regroup_weights(c):
-            wr = wraw[:].rearrange("p (c t) n -> p c t n", t=4)
-            nc.vector.tensor_copy(out=w_g[:, c, 0:384, :], in_=wr[:, c].rearrange("p t n -> p n t"))
+            rows = w_raw[:].rearrange("p (c t) n -> p c t n", t=PACK)
+            nc.vector.tensor_copy(out=w_grouped[:, c, 0:N_QKV, :], in_=rows[:, c].rearrange("p t n -> p n t"))
 
-        def quant_weights():
+        def quantise_weights():
             nc.vector.quantize_mx(
-                out=w_c[:].bitcast(FP8X4), scales=w_s[:], in_=w_g[:].rearrange("p c n t -> p (c n t)")
+                out=w_codes[:].bitcast(FP8X4),
+                scales=w_scales[:],
+                in_=w_grouped[:].rearrange("p c n t -> p (c n t)"),
             )
 
-        def stat_cols(tau):
-            i = tau % 2
-            return (i, i + 1) if tau < 2 else (0, 2)
-
-        def sumsq(tau):
+        def sum_squares(tau):
             g, jj = divmod(tau, GROUP)
             m, i = divmod(tau, 2)
             if i == 0:
-                ss[m] = small.tile([P, 2], F32, name="ss")
-                rstd[m] = small.tile([P, 2], F32, name="rstd")
+                sumsq_pair[m] = small.tile([P, 2], F32, name="ss")
+                rrms_pair[m] = small.tile([P, 2], F32, name="rstd")
             junk = junkp.tile([P, D], BF16, name="junk")
             nc.scalar.activation(
-                out=junk[:], in_=xg[g][:, jj, :], func=ACT.Square, accum_out=ss[m][:, i : i + 1]
+                out=junk[:], in_=x_group[g][:, jj, :], func=ACT.Square, accum_out=sumsq_pair[m][:, i : i + 1]
             )
 
-        def rms(tau):
+        def reciprocal_rms(tau):
             m, i = divmod(tau, 2)
-            if tau < 2 or i == 1:
-                lo, hi = stat_cols(tau)
+            if tau < GROUP or i == 1:
+                lo = i if tau < GROUP else 0
                 nc.scalar.activation(
-                    out=rstd[m][:, lo:hi],
-                    in_=ss[m][:, lo:hi],
+                    out=rrms_pair[m][:, lo : i + 1],
+                    in_=sumsq_pair[m][:, lo : i + 1],
                     func=ACT.Abs_reciprocal_sqrt,
                     scale=1.0 / D,
-                    bias=eps_t[:, 0:1],
+                    bias=eps_rms[:, 0:1],
                 )
 
-        def ymul(tau):
+        def scale_x_gpsimd(tau):
             g, jj = divmod(tau, GROUP)
             m, i = divmod(tau, 2)
             y = ypool.tile([P, D], F32, name="y")
-            ys[tau] = y
+            y_tile[tau] = y
             if tau > 0:
                 nc.gpsimd.tensor_scalar(
                     out=y[:, 0:G_COLS],
-                    in0=xg[g][:, jj, 0:G_COLS],
-                    scalar1=rstd[m][:, i : i + 1],
+                    in0=x_group[g][:, jj, 0:G_COLS],
+                    scalar1=rrms_pair[m][:, i : i + 1],
                     scalar2=0.0,
                     op0=ALU.mult,
                     op1=ALU.add,
                 )
 
-        def ymul_v(tau):
+        def scale_x_vector(tau):
             g, jj = divmod(tau, GROUP)
             m, i = divmod(tau, 2)
             lo = G_COLS if tau > 0 else 0
             nc.vector.tensor_scalar(
-                out=ys[tau][:, lo:D],
-                in0=xg[g][:, jj, lo:D],
-                scalar1=rstd[m][:, i : i + 1],
+                out=y_tile[tau][:, lo:D],
+                in0=x_group[g][:, jj, lo:D],
+                scalar1=rrms_pair[m][:, i : i + 1],
                 scalar2=None,
                 op0=ALU.mult,
             )
 
-        def trans(tau):
-            for c in range(2):
-                yT = ps_t.tile([P, 4, P], F32, name="yT")
-                yts[(tau, c)] = yT
-                for t in range(4):
-                    k0 = (c * 4 + t) * P
-                    nc.tensor.transpose(out=yT[:, t, :], in_=ys[tau][:, k0 : k0 + P], identity=ident[:])
+        def transpose(tau):
+            for c in range(PASSES):
+                yT = ps_t.tile([P, PACK, P], F32, name="yT")
+                yT_bank[(tau, c)] = yT
+                for t in range(PACK):
+                    k0 = (c * PACK + t) * P
+                    nc.tensor.transpose(out=yT[:, t, :], in_=y_tile[tau][:, k0 : k0 + P], identity=ident[:])
 
-        def evac(tau):
-            grp = gpool.tile([P, 1024], BF16, name="grp", align_bytes=64)
-            grps[tau] = grp
-            for c in range(2):
+        def times_norm_w(tau):
+            h = gpool.tile([P, PASSES * P * PACK], BF16, name="grp", align_bytes=64)
+            h_tile[tau] = h
+            width = P * PACK
+            for c in range(PASSES):
                 nc.vector.tensor_tensor(
-                    out=grp[:, c * 512 : (c + 1) * 512].rearrange("p (k t) -> p k t", t=4),
-                    in0=yts[(tau, c)][:].rearrange("p t k -> p k t"),
-                    in1=w4[:, c * 4 : (c + 1) * 4].unsqueeze(1).to_broadcast([P, P, 4]),
+                    out=h[:, c * width : (c + 1) * width].rearrange("p (k t) -> p k t", t=PACK),
+                    in0=yT_bank[(tau, c)][:].rearrange("p t k -> p k t"),
+                    in1=nw_kt[:, c * PACK : (c + 1) * PACK].unsqueeze(1).to_broadcast([P, P, PACK]),
                     op=ALU.mult,
                 )
 
-        def quant(tau):
-            codes = gpool.tile([P, 256], U32, name="codes", align_bytes=64)
-            scl = gpool.tile([P, 256], U8, name="scl", align_bytes=64)
-            cds[tau] = (codes, scl)
-            nc.vector.quantize_mx(out=codes[:].bitcast(FP8X4), scales=scl[:], in_=grps[tau][:])
+        def quantise(tau):
+            codes = gpool.tile([P, PASSES * P], U32, name="codes", align_bytes=64)
+            scales = gpool.tile([P, PASSES * P], U8, name="scl", align_bytes=64)
+            h_mx[tau] = (codes, scales)
+            nc.vector.quantize_mx(out=codes[:].bitcast(FP8X4), scales=scales[:], in_=h_tile[tau][:])
 
-        def mx(tau):
-            po = ps_o.tile([P, 512], F32, name="po")
-            pos[tau] = po
-            codes, scl = cds[tau]
-            for c in range(2):
+        def project(tau):
+            qkv = ps_o.tile([P, N_PASS], F32, name="po")
+            qkv_tile[tau] = qkv
+            codes, scales = h_mx[tau]
+            for c in range(PASSES):
                 nc.tensor.matmul_mx(
-                    out=po[:],
+                    out=qkv[:],
                     lhsT=codes[:, c * P : (c + 1) * P].bitcast(FP8X4),
-                    lhsT_scale=scl[:, c * P : (c + 1) * P],
-                    rhs=w_c[:, c * 512 : (c + 1) * 512].bitcast(FP8X4),
-                    rhs_scale=w_s[:, c * 512 : (c + 1) * 512],
+                    lhsT_scale=scales[:, c * P : (c + 1) * P],
+                    rhs=w_codes[:, c * N_PASS : (c + 1) * N_PASS].bitcast(FP8X4),
+                    rhs_scale=w_scales[:, c * N_PASS : (c + 1) * N_PASS],
                     start=(c == 0),
-                    stop=(c == 1),
+                    stop=(c == PASSES - 1),
                 )
 
-        def heads(tau):
+        def head_squares_and_v(tau):
             m, i = divmod(tau, 2)
             g, jj = divmod(tau, GROUP)
+            heads = N_QK // HD
             if i == 0:
-                ssqs[m] = small.tile([P, 8], F32, name="ssq")
+                headsq_pair[m] = small.tile([P, 2 * heads], F32, name="ssq")
             if jj == 0:
-                otile[g] = opool.tile([P, 6, GROUP, HD], F32, name="otile")
-            for w in range(4):
+                out_group[g] = opool.tile([P, N_QKV // HD, GROUP, HD], F32, name="otile")
+            for w in range(heads):
                 junk2 = junkp.tile([P, HD], BF16, name="junk2")
                 nc.scalar.activation(
                     out=junk2[:],
-                    in_=pos[tau][:, w * HD : (w + 1) * HD],
+                    in_=qkv_tile[tau][:, w * HD : (w + 1) * HD],
                     func=ACT.Square,
-                    accum_out=ssqs[m][:, i * 4 + w : i * 4 + w + 1],
+                    accum_out=headsq_pair[m][:, i * heads + w : i * heads + w + 1],
                 )
             nc.scalar.copy(
-                out=otile[g][:, 4:6, jj, :], in_=pos[tau][:, 256:384].rearrange("p (w d) -> p w d", d=HD)
+                out=out_group[g][:, heads : N_QKV // HD, jj, :],
+                in_=qkv_tile[tau][:, N_QK:N_QKV].rearrange("p (w d) -> p w d", d=HD),
             )
 
-        nrm_in = {}
-
-        def clamp(m):
-            nrm_in[m] = small.tile([P, 8], F32, name="ssc")
-            nc.scalar.activation(out=nrm_in[m][:], in_=ssqs[m][:], func=ACT.Relu, bias=tiny_n[:, 0:1])
-
-        def root(m):
-            rns[m] = small.tile([P, 8], F32, name="rn")
+        def clamp_head_squares(m):
+            clamped_pair[m] = small.tile([P, 2 * N_QK // HD], F32, name="ssc")
             nc.scalar.activation(
-                out=rns[m][:], in_=nrm_in[m][:], func=ACT.Abs_reciprocal_sqrt, bias=tiny_p[:, 0:1]
+                out=clamped_pair[m][:], in_=headsq_pair[m][:], func=ACT.Relu, bias=minus_eps_sq[:, 0:1]
             )
 
-        def scale(tau):
+        def reciprocal_norms(m):
+            rnorm_pair[m] = small.tile([P, 2 * N_QK // HD], F32, name="rn")
+            nc.scalar.activation(
+                out=rnorm_pair[m][:], in_=clamped_pair[m][:], func=ACT.Abs_reciprocal_sqrt, bias=eps_sq[:, 0:1]
+            )
+
+        def normalise_q_k(tau):
             m, i = divmod(tau, 2)
             g, jj = divmod(tau, GROUP)
+            heads = N_QK // HD
             nc.vector.tensor_tensor(
-                out=otile[g][:, 0:4, jj, :],
-                in0=pos[tau][:, 0:256].rearrange("p (w d) -> p w d", d=HD),
-                in1=rns[m][:, i * 4 : (i + 1) * 4].unsqueeze(2).to_broadcast([P, 4, HD]),
+                out=out_group[g][:, 0:heads, jj, :],
+                in0=qkv_tile[tau][:, 0:N_QK].rearrange("p (w d) -> p w d", d=HD),
+                in1=rnorm_pair[m][:, i * heads : (i + 1) * heads].unsqueeze(2).to_broadcast([P, heads, HD]),
                 op=ALU.mult,
             )
 
@@ -239,48 +251,48 @@ def tile_sharedglobalattention_pa_t_kernel(tc, x, norm_w, Wq, Wk, Wv, out_0, out
             b, j0 = divmod(g * GROUP, J)
             for m in range(3):
                 nc.sync.dma_start(
-                    out=ov[m][b][:, :, j0 + lo : j0 + hi, :], in_=otile[g][:, 2 * m : 2 * m + 2, lo:hi, :]
+                    out=out_rows[m][b][:, :, j0 + lo : j0 + hi, :], in_=out_group[g][:, 2 * m : 2 * m + 2, lo:hi, :]
                 )
 
-        def ok(tau):
+        def is_tile(tau):
             return 0 <= tau < N_TILES
 
-        for n in range(-LOAD_LEAD, N_TILES + 5):
+        for n in range(-LOAD_LEAD, N_TILES + SCALE_LAG + 1):
             if (n + LOAD_LEAD) % GROUP == 0 and 0 < (n + LOAD_LEAD) // GROUP < N_GROUPS:
                 load((n + LOAD_LEAD) // GROUP)
             if n == -SUMSQ_LEAD:
-                prep_norm_w()
-            if ok(n + Y_LEAD):
-                ymul(n + Y_LEAD)
-            if ok(n + 1):
-                trans(n + 1)
-            if ok(n - 1):
-                mx(n - 1)
-            pair_done = ok(n - 2) and (n - 2) % 2 == 1
-            if ok(n - 2):
-                heads(n - 2)
+                spread_norm_w()
+            if is_tile(n + Y_LEAD):
+                scale_x_gpsimd(n + Y_LEAD)
+            if is_tile(n + TRANSPOSE_LEAD):
+                transpose(n + TRANSPOSE_LEAD)
+            if is_tile(n - MX_LAG):
+                project(n - MX_LAG)
+            pair_done = is_tile(n - HEAD_LAG) and (n - HEAD_LAG) % 2 == 1
+            if is_tile(n - HEAD_LAG):
+                head_squares_and_v(n - HEAD_LAG)
             if pair_done:
-                clamp((n - 2) // 2)
-            if ok(n + SUMSQ_LEAD - 1):
-                rms(n + SUMSQ_LEAD - 1)
-            if ok(n + SUMSQ_LEAD):
-                sumsq(n + SUMSQ_LEAD)
+                clamp_head_squares((n - HEAD_LAG) // 2)
+            if is_tile(n + SUMSQ_LEAD - 1):
+                reciprocal_rms(n + SUMSQ_LEAD - 1)
+            if is_tile(n + SUMSQ_LEAD):
+                sum_squares(n + SUMSQ_LEAD)
             if pair_done:
-                root((n - 2) // 2)
-            if ok(n):
-                evac(n)
+                reciprocal_norms((n - HEAD_LAG) // 2)
+            if is_tile(n):
+                times_norm_w(n)
             if n == 0:
-                quant_weights()
-            if ok(n - 4):
-                scale(n - 4)
-            if ok(n):
-                quant(n)
-            if ok(n + Y_LEAD):
-                ymul_v(n + Y_LEAD)
-            if n + SUMSQ_LEAD - 2 in (0, 1):
-                regroup_weights(n + SUMSQ_LEAD - 2)
-            if ok(n - 4):
-                g_out, j_out = divmod(n - 4, GROUP)
+                for c in range(PASSES):
+                    regroup_weights(c)
+                quantise_weights()
+            if is_tile(n - SCALE_LAG):
+                normalise_q_k(n - SCALE_LAG)
+            if is_tile(n):
+                quantise(n)
+            if is_tile(n + Y_LEAD):
+                scale_x_vector(n + Y_LEAD)
+            if is_tile(n - SCALE_LAG):
+                g_out, j_out = divmod(n - SCALE_LAG, GROUP)
                 if g_out < N_GROUPS - 1:
                     if j_out == GROUP - 1:
                         store(g_out, 0, GROUP)

from contextlib import ExitStack

import concourse.mybir as mybir
from concourse.masks import make_identity

F32 = mybir.dt.float32
BF16 = mybir.dt.bfloat16
U32 = mybir.dt.uint32
U8 = mybir.dt.uint8
FP8X4 = mybir.dt.float8_e4m3fn_x4
ACT = mybir.ActivationFunctionType
ALU = mybir.AluOpType

P = 128
PACK = 4
B, L, D = 4, 2048, 1024
HD = 64
N_QK = 256
N_QKV = 384
N_PASS = 512
PASSES = D // (P * PACK)
CHUNKS = D // P
J = L // P
GROUP = 4
N_TILES = B * J
N_GROUPS = N_TILES // GROUP
FLOPS = 2 * B * L * D * N_QKV

LOAD_LEAD = 11
SUMSQ_LEAD = 7
Y_LEAD = 3
TRANSPOSE_LEAD = 1
MX_LAG = 1
HEAD_LAG = 2
SCALE_LAG = 4
G_COLS = 704


def tile_sharedglobalattention_pa_t_kernel(tc, x, norm_w, Wq, Wk, Wv, out_0, out_1, out_2):
    nc = tc.nc
    with ExitStack() as ctx:
        const = ctx.enter_context(tc.tile_pool(name="const", bufs=1))
        xpool = ctx.enter_context(tc.tile_pool(name="xin", bufs=4))
        junkp = ctx.enter_context(tc.tile_pool(name="junk", bufs=2))
        small = ctx.enter_context(tc.tile_pool(name="small", bufs=8))
        ypool = ctx.enter_context(tc.tile_pool(name="ytok", bufs=5))
        gpool = ctx.enter_context(tc.tile_pool(name="grouped", bufs=3))
        opool = ctx.enter_context(tc.tile_pool(name="outs", bufs=3))
        ps_t = ctx.enter_context(tc.psum_pool(name="ps_t", bufs=4))
        ps_o = ctx.enter_context(tc.psum_pool(name="ps_o", bufs=4))
        ctx.enter_context(tc.manual_schedule())

        x_rows = [x[b].rearrange("(p j) d -> p j d", j=J) for b in range(B)]
        out_rows = [[o[b].rearrange("n (p j) d -> p n j d", j=J) for b in range(B)] for o in (out_0, out_1, out_2)]

        x_group, sumsq_pair, rrms_pair, y_tile, yT_bank, h_tile, h_mx = {}, {}, {}, {}, {}, {}, {}
        qkv_tile, headsq_pair, clamped_pair, rnorm_pair, out_group = {}, {}, {}, {}, {}

        nw8 = const.tile([CHUNKS, P], BF16, name="nw8")

        def load(g):
            b, j0 = divmod(g * GROUP, J)
            t = xpool.tile([P, GROUP, D], BF16, name="xg")
            x_group[g] = t
            if g == 0:
                for jj in range(GROUP):
                    nc.sync.dma_start(out=t[:, jj : jj + 1, :], in_=x_rows[b][:, j0 + jj : j0 + jj + 1, :])
                    if jj == 0:
                        nc.sync.dma_start(out=nw8[:], in_=norm_w.rearrange("(c p) -> c p", p=P))
            else:
                nc.sync.dma_start(out=t[:], in_=x_rows[b][:, j0 : j0 + GROUP, :])

        load(0)

        w_raw = const.tile([P, CHUNKS, N_QKV], BF16, name="wraw")
        for m, w in enumerate((Wq, Wk, Wv)):
            nc.scalar.dma_start(
                out=w_raw[:, :, m * P : (m + 1) * P], in_=w.rearrange("(c p) n -> p c n", p=P)
            )
        nw_rows = const.tile([P, P], F32, name="nw_f")
        nc.vector.memset(nw_rows[:], 0.0)
        eps_rms = const.tile([P, 1], F32, name="eps_t")
        nc.vector.memset(eps_rms[:], 1e-6)
        eps_sq = const.tile([P, 1], F32, name="tiny_p")
        nc.vector.memset(eps_sq[:], 1e-24)
        minus_eps_sq = const.tile([P, 1], F32, name="tiny_n")
        nc.vector.memset(minus_eps_sq[:], -1e-24)
        warm = const.tile([P, 1], F32, name="warm")
        nc.scalar.activation(out=warm[:], in_=eps_rms[:], func=ACT.Abs_reciprocal_sqrt)
        ident = const.tile([P, P], F32, name="ident")
        make_identity(nc, ident[:])
        w_grouped = const.tile([P, PASSES, N_PASS, PACK], BF16, name="w_g", align_bytes=64)
        nc.gpsimd.memset(w_grouped[:, :, N_QKV:N_PASS, :], 0.0)
        w_codes = const.tile([P, PASSES * N_PASS], U32, name="w_c", align_bytes=64)
        w_scales = const.tile([P, PASSES * N_PASS], U8, name="w_s", align_bytes=64)
        nw_kt = const.tile([P, CHUNKS], F32, name="w4")

        def spread_norm_w():
            nc.vector.tensor_copy(out=nw_rows[0:CHUNKS, :], in_=nw8[:])
            nw_ps = ps_t.tile([P, PACK, P], F32, name="yT")
            nc.tensor.transpose(out=nw_ps[:, 0, :], in_=nw_rows[:], identity=ident[:])
            nc.vector.tensor_copy(out=nw_kt[:], in_=nw_ps[:, 0, 0:CHUNKS])

        def regroup_weights(c):
            rows = w_raw[:].rearrange("p (c t) n -> p c t n", t=PACK)
            nc.vector.tensor_copy(out=w_grouped[:, c, 0:N_QKV, :], in_=rows[:, c].rearrange("p t n -> p n t"))

        def quantise_weights():
            nc.vector.quantize_mx(
                out=w_codes[:].bitcast(FP8X4),
                scales=w_scales[:],
                in_=w_grouped[:].rearrange("p c n t -> p (c n t)"),
            )

        def sum_squares(tau):
            g, jj = divmod(tau, GROUP)
            m, i = divmod(tau, 2)
            if i == 0:
                sumsq_pair[m] = small.tile([P, 2], F32, name="ss")
                rrms_pair[m] = small.tile([P, 2], F32, name="rstd")
            junk = junkp.tile([P, D], BF16, name="junk")
            nc.scalar.activation(
                out=junk[:], in_=x_group[g][:, jj, :], func=ACT.Square, accum_out=sumsq_pair[m][:, i : i + 1]
            )

        def reciprocal_rms(tau):
            m, i = divmod(tau, 2)
            if tau < GROUP or i == 1:
                lo = i if tau < GROUP else 0
                nc.scalar.activation(
                    out=rrms_pair[m][:, lo : i + 1],
                    in_=sumsq_pair[m][:, lo : i + 1],
                    func=ACT.Abs_reciprocal_sqrt,
                    scale=1.0 / D,
                    bias=eps_rms[:, 0:1],
                )

        def scale_x_gpsimd(tau):
            g, jj = divmod(tau, GROUP)
            m, i = divmod(tau, 2)
            y = ypool.tile([P, D], F32, name="y")
            y_tile[tau] = y
            if tau > 0:
                nc.gpsimd.tensor_scalar(
                    out=y[:, 0:G_COLS],
                    in0=x_group[g][:, jj, 0:G_COLS],
                    scalar1=rrms_pair[m][:, i : i + 1],
                    scalar2=0.0,
                    op0=ALU.mult,
                    op1=ALU.add,
                )

        def scale_x_vector(tau):
            g, jj = divmod(tau, GROUP)
            m, i = divmod(tau, 2)
            lo = G_COLS if tau > 0 else 0
            nc.vector.tensor_scalar(
                out=y_tile[tau][:, lo:D],
                in0=x_group[g][:, jj, lo:D],
                scalar1=rrms_pair[m][:, i : i + 1],
                scalar2=None,
                op0=ALU.mult,
            )

        def transpose(tau):
            for c in range(PASSES):
                yT = ps_t.tile([P, PACK, P], F32, name="yT")
                yT_bank[(tau, c)] = yT
                for t in range(PACK):
                    k0 = (c * PACK + t) * P
                    nc.tensor.transpose(out=yT[:, t, :], in_=y_tile[tau][:, k0 : k0 + P], identity=ident[:])

        def times_norm_w(tau):
            h = gpool.tile([P, PASSES * P * PACK], BF16, name="grp", align_bytes=64)
            h_tile[tau] = h
            width = P * PACK
            for c in range(PASSES):
                nc.vector.tensor_tensor(
                    out=h[:, c * width : (c + 1) * width].rearrange("p (k t) -> p k t", t=PACK),
                    in0=yT_bank[(tau, c)][:].rearrange("p t k -> p k t"),
                    in1=nw_kt[:, c * PACK : (c + 1) * PACK].unsqueeze(1).to_broadcast([P, P, PACK]),
                    op=ALU.mult,
                )

        def quantise(tau):
            codes = gpool.tile([P, PASSES * P], U32, name="codes", align_bytes=64)
            scales = gpool.tile([P, PASSES * P], U8, name="scl", align_bytes=64)
            h_mx[tau] = (codes, scales)
            nc.vector.quantize_mx(out=codes[:].bitcast(FP8X4), scales=scales[:], in_=h_tile[tau][:])

        def project(tau):
            qkv = ps_o.tile([P, N_PASS], F32, name="po")
            qkv_tile[tau] = qkv
            codes, scales = h_mx[tau]
            for c in range(PASSES):
                nc.tensor.matmul_mx(
                    out=qkv[:],
                    lhsT=codes[:, c * P : (c + 1) * P].bitcast(FP8X4),
                    lhsT_scale=scales[:, c * P : (c + 1) * P],
                    rhs=w_codes[:, c * N_PASS : (c + 1) * N_PASS].bitcast(FP8X4),
                    rhs_scale=w_scales[:, c * N_PASS : (c + 1) * N_PASS],
                    start=(c == 0),
                    stop=(c == PASSES - 1),
                )

        def head_squares_and_v(tau):
            m, i = divmod(tau, 2)
            g, jj = divmod(tau, GROUP)
            heads = N_QK // HD
            if i == 0:
                headsq_pair[m] = small.tile([P, 2 * heads], F32, name="ssq")
            if jj == 0:
                out_group[g] = opool.tile([P, N_QKV // HD, GROUP, HD], F32, name="otile")
            for w in range(heads):
                junk2 = junkp.tile([P, HD], BF16, name="junk2")
                nc.scalar.activation(
                    out=junk2[:],
                    in_=qkv_tile[tau][:, w * HD : (w + 1) * HD],
                    func=ACT.Square,
                    accum_out=headsq_pair[m][:, i * heads + w : i * heads + w + 1],
                )
            nc.scalar.copy(
                out=out_group[g][:, heads : N_QKV // HD, jj, :],
                in_=qkv_tile[tau][:, N_QK:N_QKV].rearrange("p (w d) -> p w d", d=HD),
            )

        def clamp_head_squares(m):
            clamped_pair[m] = small.tile([P, 2 * N_QK // HD], F32, name="ssc")
            nc.scalar.activation(
                out=clamped_pair[m][:], in_=headsq_pair[m][:], func=ACT.Relu, bias=minus_eps_sq[:, 0:1]
            )

        def reciprocal_norms(m):
            rnorm_pair[m] = small.tile([P, 2 * N_QK // HD], F32, name="rn")
            nc.scalar.activation(
                out=rnorm_pair[m][:], in_=clamped_pair[m][:], func=ACT.Abs_reciprocal_sqrt, bias=eps_sq[:, 0:1]
            )

        def normalise_q_k(tau):
            m, i = divmod(tau, 2)
            g, jj = divmod(tau, GROUP)
            heads = N_QK // HD
            nc.vector.tensor_tensor(
                out=out_group[g][:, 0:heads, jj, :],
                in0=qkv_tile[tau][:, 0:N_QK].rearrange("p (w d) -> p w d", d=HD),
                in1=rnorm_pair[m][:, i * heads : (i + 1) * heads].unsqueeze(2).to_broadcast([P, heads, HD]),
                op=ALU.mult,
            )

        def store(g, lo, hi):
            b, j0 = divmod(g * GROUP, J)
            for m in range(3):
                nc.sync.dma_start(
                    out=out_rows[m][b][:, :, j0 + lo : j0 + hi, :], in_=out_group[g][:, 2 * m : 2 * m + 2, lo:hi, :]
                )

        def is_tile(tau):
            return 0 <= tau < N_TILES

        for n in range(-LOAD_LEAD, N_TILES + SCALE_LAG + 1):
            if (n + LOAD_LEAD) % GROUP == 0 and 0 < (n + LOAD_LEAD) // GROUP < N_GROUPS:
                load((n + LOAD_LEAD) // GROUP)
            if n == -SUMSQ_LEAD:
                spread_norm_w()
            if is_tile(n + Y_LEAD):
                scale_x_gpsimd(n + Y_LEAD)
            if is_tile(n + TRANSPOSE_LEAD):
                transpose(n + TRANSPOSE_LEAD)
            if is_tile(n - MX_LAG):
                project(n - MX_LAG)
            pair_done = is_tile(n - HEAD_LAG) and (n - HEAD_LAG) % 2 == 1
            if is_tile(n - HEAD_LAG):
                head_squares_and_v(n - HEAD_LAG)
            if pair_done:
                clamp_head_squares((n - HEAD_LAG) // 2)
            if is_tile(n + SUMSQ_LEAD - 1):
                reciprocal_rms(n + SUMSQ_LEAD - 1)
            if is_tile(n + SUMSQ_LEAD):
                sum_squares(n + SUMSQ_LEAD)
            if pair_done:
                reciprocal_norms((n - HEAD_LAG) // 2)
            if is_tile(n):
                times_norm_w(n)
            if n == 0:
                for c in range(PASSES):
                    regroup_weights(c)
                quantise_weights()
            if is_tile(n - SCALE_LAG):
                normalise_q_k(n - SCALE_LAG)
            if is_tile(n):
                quantise(n)
            if is_tile(n + Y_LEAD):
                scale_x_vector(n + Y_LEAD)
            if is_tile(n - SCALE_LAG):
                g_out, j_out = divmod(n - SCALE_LAG, GROUP)
                if g_out < N_GROUPS - 1:
                    if j_out == GROUP - 1:
                        store(g_out, 0, GROUP)
                elif j_out % 2 == 1:
                    store(g_out, j_out - 1, j_out + 1)
